import numpy as np
import ml_dtypes


def mxq(x, axis, fmt="e4m3"):
    dtype, down = {"e4m3": (ml_dtypes.float8_e4m3fn, 7), "e5m2": (ml_dtypes.float8_e5m2, 14)}[fmt]
    v = np.moveaxis(np.asarray(x, np.float32).astype(ml_dtypes.bfloat16).astype(np.float64), axis, -1)
    blocks = v.reshape(v.shape[:-1] + (-1, 32))
    amax = np.abs(blocks).max(-1, keepdims=True)
    byte = np.maximum(np.where(amax > 0, np.frexp(amax)[1] - 1 + 127, 0) - down, 1)
    scale = np.exp2(byte - 127.0)
    codes = (blocks / scale).astype(np.float32).astype(dtype).astype(np.float64)
    return np.moveaxis((codes * scale).reshape(v.shape), -1, axis)


WIDE = False


def mx_kscale(k):
    if not WIDE:
        return np.ones(k)
    levels = np.array([10, -10, 5, -5, 0])
    a = np.random.permutation(np.resize(levels, k // 512 * 4)).reshape(k // 512, 4)
    idx = np.arange(k)
    return np.exp2(a[idx // 512, idx % 128 // 32])


BF16 = ml_dtypes.bfloat16


def bf(x):
    return np.asarray(x, np.float32).astype(BF16)


def f64(x):
    return np.asarray(x).astype(np.float64)


E2M1 = np.array([0.0, 0.5, 1.0, 1.5, 2.0, 3.0, 4.0, 6.0, -0.0, -0.5, -1.0, -1.5, -2.0, -3.0, -4.0, -6.0])


def pack_weight(w, fmt):
    k, n = w.shape
    w = f64(bf(w)).reshape(k // 32, 32, n)
    amax = np.abs(w).max(1)
    if fmt == "e4m3":
        byte = np.frexp(amax)[1] - 1 + 127 - 7
    else:
        mant, ex = np.frexp(amax / 6.0)
        byte = np.where(mant > 0.5, ex, ex - 1) + 127
    byte = np.clip(np.where(amax > 0, byte, 1), 1, 254)
    scaled = (w * np.exp2(127.0 - byte)[:, None, :]).reshape(k, n).astype(np.float32)
    by_word = np.ascontiguousarray(scaled.reshape(k // 512, 128, 4, n).transpose(0, 1, 3, 2))
    if fmt == "e4m3":
        words = by_word.astype(ml_dtypes.float8_e4m3fn).view(np.uint8)
    else:
        c = by_word.astype(ml_dtypes.float4_e2m1fn).view(np.uint8) & 0xF
        words = c[..., 0::2] | (c[..., 1::2] << 4)
    return np.ascontiguousarray(words), np.ascontiguousarray(byte.astype(np.uint8).reshape(k // 512, 16, n))


def unpack_weight(words, scales, fmt):
    g, p, n, _ = words.shape
    if fmt == "e4m3":
        vals = np.ascontiguousarray(words).view(ml_dtypes.float8_e4m3fn).astype(np.float64)
    else:
        nib = np.empty((g, p, n, 4), np.uint8)
        nib[..., 0::2] = words & 0xF
        nib[..., 1::2] = words >> 4
        vals = E2M1[nib]
    vals = vals * np.repeat(np.exp2(scales.astype(np.float64) - 127.0), 8, axis=1)[..., None]
    return vals.transpose(0, 1, 3, 2).reshape(g * 512, n)


B, IN, OUT = 512, 2048, 2048


def setup_inputs():
    s = mx_kscale(IN)
    input_data = bf(np.random.standard_normal((B, IN)) * s)
    weight_words, weight_scales = pack_weight((np.random.standard_normal((OUT, IN)) / np.sqrt(IN) / s).T, "e4m3")
    return {"input_data": input_data,
            "weight_words": weight_words,
            "weight_scales": weight_scales,
            "bias": bf(np.random.standard_normal(OUT) * 0.5),
            "prev_grad": bf(np.random.standard_normal((OUT, IN)) / np.sqrt(IN) / s),
            "prev_bias_grad": bf(np.random.standard_normal(OUT) * 0.5),
            "lr_samples": bf(np.random.uniform(0.1, 1.0, B))}


def reference(input_data, weight_words, weight_scales, bias, prev_grad, prev_bias_grad, lr_samples):
    xq = mxq(f64(input_data), 1, "e4m3")
    base = (xq @ unpack_weight(weight_words, weight_scales, "e4m3")) + f64(bias)
    pert = (xq @ mxq(f64(prev_grad), 1, "e4m3").T) + f64(prev_bias_grad)
    return base - f64(lr_samples)[:, None] * pert

@@ -1,0 +1,200 @@
+from contextlib import ExitStack
+
+import concourse.mybir as mybir
+from concourse.masks import make_identity
+
+F32 = mybir.dt.float32
+BF16 = mybir.dt.bfloat16
+I32 = mybir.dt.int32
+U32 = mybir.dt.uint32
+U8 = mybir.dt.uint8
+FP8X4 = mybir.dt.float8_e4m3fn_x4
+ADD = mybir.AluOpType.add
+MULT = mybir.AluOpType.mult
+
+P = 128
+PACK = 4
+K_PASS = P * PACK
+BATCH, K, N = 512, 2048, 2048
+PASSES = K // K_PASS
+PAIR = 2 * P
+X_PAIRS = BATCH // PAIR
+G_PAIRS = N // PAIR
+N_TILE = 512
+N_TILES = N // N_TILE
+WORDS_PASS = K_PASS // 2
+
+FLOPS = 2 * 2 * BATCH * K * N
+
+
+def quantise_pair_along_k(nc, banks, stage, ident, raw, codes, scales):
+    words = raw[:].bitcast(F32)
+    bank_of_pass = [banks.tile([P, 2, 2, P], F32, name="bank") for g in range(PASSES)]
+    for a in range(2):
+        for g in range(PASSES):
+            for u in range(2):
+                nc.tensor.transpose(
+                    bank_of_pass[g][:, a, u, :],
+                    words[:, a, WORDS_PASS * g + u : WORDS_PASS * (g + 1) : 2],
+                    ident[:],
+                )
+    for g in range(PASSES):
+        grouped = stage.tile([P, PAIR, PACK], BF16, align_bytes=64)
+        nc.scalar.copy(
+            out=grouped[:].bitcast(F32).rearrange("p (a r) u -> p a r u", a=2),
+            in_=bank_of_pass[g][:].rearrange("p a u r -> p a r u"),
+        )
+        nc.vector.quantize_mx(
+            out=codes[:, g, :].bitcast(FP8X4),
+            scales=scales[:, g, :],
+            in_=grouped[:].rearrange("p r t -> p (r t)"),
+        )
+
+
+def tile_optimizedlinear_kernel(
+    tc, input_data, weight_words, weight_scales, bias, prev_grad, prev_bias_grad, lr_samples, out
+):
+    nc = tc.nc
+    with ExitStack() as ctx:
+        keep = ctx.enter_context(tc.tile_pool(name="keep", bufs=1))
+        stage = ctx.enter_context(tc.tile_pool(name="stage", bufs=8))
+        quantised = ctx.enter_context(tc.tile_pool(name="quantised", bufs=3))
+        banks = ctx.enter_context(tc.psum_pool(name="banks", bufs=4))
+        sums = ctx.enter_context(tc.psum_pool(name="sums", bufs=4))
+        ctx.enter_context(tc.manual_schedule())
+
+        ident = keep.tile([P, P], F32)
+        make_identity(nc, ident[:])
+        w_planes = keep.tile([P, N], U8, align_bytes=64)
+        nc.vector.memset(w_planes[:].bitcast(I32), 0)
+        lr_rows = keep.tile([P, BATCH], BF16)
+        vec_rows = keep.tile([P, N], BF16)
+        nc.vector.memset(lr_rows[:], 0.0)
+        nc.vector.memset(vec_rows[:], 0.0)
+        nc.vector.memset(lr_rows[0:1, :], 1.0)
+
+        x_raw = [keep.tile([P, 2, K], BF16, name="x_raw%d" % h) for h in range(X_PAIRS)]
+        g_raw = [keep.tile([P, 2, K], BF16, name="g_raw%d" % i) for i in range(G_PAIRS)]
+        w_words = [keep.tile([P, PASSES, N_TILE], U32, name="w_words%d" % j, align_bytes=64) for j in range(N_TILES)]
+
+        def load_g(i):
+            rows = prev_grad[PAIR * i : PAIR * (i + 1), :]
+            nc.sync.dma_start(out=g_raw[i][:], in_=rows.rearrange("(a p) k -> p a k", p=P))
+
+        def load_w(j):
+            cols = weight_words.rearrange("g p n t -> p g (n t)")[:, :, PACK * N_TILE * j : PACK * N_TILE * (j + 1)]
+            nc.sync.dma_start(out=w_words[j][:].bitcast(I32), in_=cols.bitcast(I32))
+
+        for h in range(X_PAIRS):
+            for a in range(2):
+                m = 2 * h + a
+                nc.sync.dma_start(out=x_raw[h][:, a, :], in_=input_data[P * m : P * (m + 1), :])
+        load_g(0)
+        for quadrant in range(4):
+            nc.sync.dma_start(
+                out=w_planes[32 * quadrant : 32 * quadrant + 16, :].bitcast(I32),
+                in_=weight_scales[:, 4 * quadrant : 4 * quadrant + 4, :].bitcast(I32),
+            )
+        load_w(0)
+        for j in range(1, N_TILES):
+            load_g(2 * j - 1)
+            load_g(2 * j)
+            load_w(j)
+        load_g(G_PAIRS - 1)
+
+        nc.scalar.dma_start(out=vec_rows[0:1, :], in_=bias.unsqueeze(0))
+        nc.scalar.dma_start(out=vec_rows[32:33, :], in_=prev_bias_grad.unsqueeze(0))
+        nc.scalar.dma_start(out=lr_rows[32:33, :], in_=lr_samples.unsqueeze(0))
+        lr_col = keep.tile([P, BATCH // P], BF16)
+        with nc.allow_non_contiguous_dma(reason="512 learning rates, one batch row to a partition"):
+            nc.scalar.dma_start(out=lr_col[:], in_=lr_samples.rearrange("(m p) -> p m", p=P))
+        nc.vector.tensor_scalar_mul(out=lr_rows[32:64, :], in0=lr_rows[32:64, :], scalar1=-1.0)
+        neg_lr = keep.tile([P, BATCH // P], F32)
+        nc.vector.tensor_scalar_mul(out=neg_lr[:], in0=lr_col[:], scalar1=-1.0)
+
+        x_codes = [keep.tile([P, PASSES, PAIR], U32, name="x_codes%d" % h, align_bytes=64) for h in range(X_PAIRS)]
+        x_scales = [keep.tile([P, PASSES, PAIR], U8, name="x_scales%d" % h, align_bytes=64) for h in range(X_PAIRS)]
+        for h in range(X_PAIRS):
+            quantise_pair_along_k(nc, banks, stage, ident, x_raw[h], x_codes[h], x_scales[h])
+
+        result = [
+            [keep.tile([P, N_TILE], F32, name="result%d_%d" % (m, j)) for j in range(N_TILES)]
+            for m in range(BATCH // P)
+        ]
+
+        def x_operand(m, g):
+            rows = slice(P * (m % 2), P * (m % 2 + 1))
+            return x_codes[m // 2][:, g, rows].bitcast(FP8X4), x_scales[m // 2][:, g, rows]
+
+        def bias_terms(m, j):
+            terms = sums.tile([P, N_TILE], F32, name="sum")
+            nc.tensor.matmul(
+                out=terms[:],
+                lhsT=lr_rows[:, P * m : P * (m + 1)],
+                rhs=vec_rows[:, N_TILE * j : N_TILE * (j + 1)],
+                start=True,
+                stop=True,
+            )
+            nc.scalar.copy(out=result[m][j][:], in_=terms[:])
+
+        def base_product(m, j):
+            base = sums.tile([P, N_TILE], F32, name="sum")
+            for g in range(PASSES):
+                x_words, x_plane = x_operand(m, g)
+                nc.tensor.matmul_mx(
+                    out=base[:],
+                    lhsT=x_words,
+                    lhsT_scale=x_plane,
+                    rhs=w_words[j][:, g, :].bitcast(FP8X4),
+                    rhs_scale=w_planes[4 * g : P, N_TILE * j : N_TILE * (j + 1)],
+                    start=(g == 0),
+                    stop=(g == PASSES - 1),
+                )
+            nc.vector.tensor_tensor(out=result[m][j][:], in0=base[:], in1=result[m][j][:], op=ADD)
+
+        def pert_product(i, g_codes, g_scales):
+            j = i // 2
+            cols = slice(PAIR * (i % 2), PAIR * (i % 2 + 1))
+            for h in range(X_PAIRS):
+                pert = sums.tile([P, 2, PAIR], F32, name="sum")
+                for a in range(2):
+                    for g in range(PASSES):
+                        x_words, x_plane = x_operand(2 * h + a, g)
+                        nc.tensor.matmul_mx(
+                            out=pert[:, a, :],
+                            lhsT=x_words,
+                            lhsT_scale=x_plane,
+                            rhs=g_codes[:, g, :].bitcast(FP8X4),
+                            rhs_scale=g_scales[:, g, :],
+                            start=(g == 0),
+                            stop=(g == PASSES - 1),
+                        )
+                for a in range(2):
+                    m = 2 * h + a
+                    nc.vector.scalar_tensor_tensor(
+                        out=result[m][j][:, cols],
+                        in0=pert[:, a, :],
+                        scalar=neg_lr[:, m : m + 1],
+                        in1=result[m][j][:, cols],
+                        op0=MULT,
+                        op1=ADD,
+                    )
+                    if i % 2 == 1:
+                        nc.sync.dma_start(
+                            out=out[P * m : P * (m + 1), N_TILE * j : N_TILE * (j + 1)], in_=result[m][j][:]
+                        )
+
+        previous = None
+        for i in range(G_PAIRS):
+            j = i // 2
+            for m in (2 * (i % 2), 2 * (i % 2) + 1):
+                bias_terms(m, j)
+            g_codes = quantised.tile([P, PASSES, PAIR], U32, align_bytes=64)
+            g_scales = quantised.tile([P, PASSES, PAIR], U8, align_bytes=64)
+            quantise_pair_along_k(nc, banks, stage, ident, g_raw[i], g_codes, g_scales)
+            for m in (2 * (i % 2), 2 * (i % 2) + 1):
+                base_product(m, j)
+            if previous is not None:
+                pert_product(i - 1, previous[0], previous[1])
+            previous = (g_codes, g_scales)
+        pert_product(G_PAIRS - 1, previous[0], previous[1])

@@ -22,22 +22,23 @@ X_PAIRS = BATCH // PAIR
 G_PAIRS = N // PAIR
 N_TILE = 512
 N_TILES = N // N_TILE
-WORDS_PASS = K_PASS // 2
+HALVES = 2 * N_TILES
+BASE_LEAD = 2
+PERT_LAG = 2
 
 FLOPS = 2 * 2 * BATCH * K * N
 
 
-def quantise_pair_along_k(nc, banks, stage, ident, raw, codes, scales):
-    words = raw[:].bitcast(F32)
+def by_half(raw):
+    return raw[:].bitcast(F32).rearrange("p a (g i u) -> p a g u i", g=PASSES, u=2)
+
+
+def quantise_pair_along_k(nc, banks, stage, ident, halves, codes, scales):
     bank_of_pass = [banks.tile([P, 2, 2, P], F32, name="bank") for g in range(PASSES)]
     for a in range(2):
         for g in range(PASSES):
             for u in range(2):
-                nc.tensor.transpose(
-                    bank_of_pass[g][:, a, u, :],
-                    words[:, a, WORDS_PASS * g + u : WORDS_PASS * (g + 1) : 2],
-                    ident[:],
-                )
+                nc.tensor.transpose(bank_of_pass[g][:, a, u, :], halves[:, a, g, u, :], ident[:])
     for g in range(PASSES):
         grouped = stage.tile([P, PAIR, PACK], BF16, align_bytes=64)
         nc.scalar.copy(
@@ -58,7 +59,8 @@ def tile_optimizedlinear_kernel(
     with ExitStack() as ctx:
         keep = ctx.enter_context(tc.tile_pool(name="keep", bufs=1))
         stage = ctx.enter_context(tc.tile_pool(name="stage", bufs=8))
-        quantised = ctx.enter_context(tc.tile_pool(name="quantised", bufs=3))
+        sorting = ctx.enter_context(tc.tile_pool(name="sorting", bufs=2))
+        quantised = ctx.enter_context(tc.tile_pool(name="quantised", bufs=PERT_LAG + 2))
         banks = ctx.enter_context(tc.psum_pool(name="banks", bufs=4))
         sums = ctx.enter_context(tc.psum_pool(name="sums", bufs=4))
         ctx.enter_context(tc.manual_schedule())
@@ -89,18 +91,15 @@ def tile_optimizedlinear_kernel(
             for a in range(2):
                 m = 2 * h + a
                 nc.sync.dma_start(out=x_raw[h][:, a, :], in_=input_data[P * m : P * (m + 1), :])
-        load_g(0)
         for quadrant in range(4):
             nc.sync.dma_start(
                 out=w_planes[32 * quadrant : 32 * quadrant + 16, :].bitcast(I32),
                 in_=weight_scales[:, 4 * quadrant : 4 * quadrant + 4, :].bitcast(I32),
             )
-        load_w(0)
-        for j in range(1, N_TILES):
-            load_g(2 * j - 1)
-            load_g(2 * j)
+        for j in range(N_TILES):
             load_w(j)
-        load_g(G_PAIRS - 1)
+            load_g(2 * j)
+            load_g(2 * j + 1)
 
         nc.scalar.dma_start(out=vec_rows[0:1, :], in_=bias.unsqueeze(0))
         nc.scalar.dma_start(out=vec_rows[32:33, :], in_=prev_bias_grad.unsqueeze(0))
@@ -115,7 +114,7 @@ def tile_optimizedlinear_kernel(
         x_codes = [keep.tile([P, PASSES, PAIR], U32, name="x_codes%d" % h, align_bytes=64) for h in range(X_PAIRS)]
         x_scales = [keep.tile([P, PASSES, PAIR], U8, name="x_scales%d" % h, align_bytes=64) for h in range(X_PAIRS)]
         for h in range(X_PAIRS):
-            quantise_pair_along_k(nc, banks, stage, ident, x_raw[h], x_codes[h], x_scales[h])
+            quantise_pair_along_k(nc, banks, stage, ident, by_half(x_raw[h]), x_codes[h], x_scales[h])
 
         result = [
             [keep.tile([P, N_TILE], F32, name="result%d_%d" % (m, j)) for j in range(N_TILES)]
@@ -184,17 +183,46 @@ def tile_optimizedlinear_kernel(
                             out=out[P * m : P * (m + 1), N_TILE * j : N_TILE * (j + 1)], in_=result[m][j][:]
                         )
 
-        previous = None
-        for i in range(G_PAIRS):
-            j = i // 2
-            for m in (2 * (i % 2), 2 * (i % 2) + 1):
+        def rows_and_tile(half):
+            return (2 * (half % 2), 2 * (half % 2) + 1), half // 2
+
+        def bias_terms_of(half):
+            rows, j = rows_and_tile(half)
+            for m in rows:
                 bias_terms(m, j)
-            g_codes = quantised.tile([P, PASSES, PAIR], U32, align_bytes=64)
-            g_scales = quantised.tile([P, PASSES, PAIR], U8, align_bytes=64)
-            quantise_pair_along_k(nc, banks, stage, ident, g_raw[i], g_codes, g_scales)
-            for m in (2 * (i % 2), 2 * (i % 2) + 1):
+
+        def base_product_of(half):
+            rows, j = rows_and_tile(half)
+            for m in rows:
                 base_product(m, j)
-            if previous is not None:
-                pert_product(i - 1, previous[0], previous[1])
-            previous = (g_codes, g_scales)
-        pert_product(G_PAIRS - 1, previous[0], previous[1])
+
+        def sort_words(i):
+            halves = sorting.tile([P, 2, PASSES, 2, P], F32, name="halves")
+            nc.vector.tensor_copy(out=halves[:, 0, :, :, :], in_=by_half(g_raw[i])[:, 0, :, :, :])
+            nc.scalar.copy(out=halves[:, 1, :, :, :], in_=by_half(g_raw[i])[:, 1, :, :, :])
+            return halves
+
+        for half in range(BASE_LEAD):
+            bias_terms_of(half)
+        base_product_of(0)
+        halves = sort_words(0)
+        for half in range(1, BASE_LEAD):
+            base_product_of(half)
+
+        g_quantised = []
+        for i in range(G_PAIRS + PERT_LAG):
+            half = i + BASE_LEAD
+            if half < HALVES:
+                bias_terms_of(half)
+            if i < G_PAIRS:
+                sorted_now = halves
+                if i + 1 < G_PAIRS:
+                    halves = sort_words(i + 1)
+                g_codes = quantised.tile([P, PASSES, PAIR], U32, align_bytes=64)
+                g_scales = quantised.tile([P, PASSES, PAIR], U8, align_bytes=64)
+                quantise_pair_along_k(nc, banks, stage, ident, sorted_now, g_codes, g_scales)
+                g_quantised.append((g_codes, g_scales))
+            if i >= PERT_LAG:
+                pert_product(i - PERT_LAG, g_quantised[i - PERT_LAG][0], g_quantised[i - PERT_LAG][1])
+            if half < HALVES:
+                base_product_of(half)

@@ -22,34 +22,40 @@ X_PAIRS = BATCH // PAIR
 G_PAIRS = N // PAIR
 N_TILE = 512
 N_TILES = N // N_TILE
-HALVES = 2 * N_TILES
+PORTIONS = 2 * N_TILES
 BASE_LEAD = 2
 PERT_LAG = 2
 
 FLOPS = 2 * 2 * BATCH * K * N
 
 
-def by_half(raw):
+def words_by_half(raw):
     return raw[:].bitcast(F32).rearrange("p a (g i u) -> p a g u i", g=PASSES, u=2)
 
 
-def quantise_pair_along_k(nc, banks, stage, ident, halves, codes, scales):
+def transpose_pair(nc, banks, stage, ident, words, vector_helps):
     bank_of_pass = [banks.tile([P, 2, 2, P], F32, name="bank") for g in range(PASSES)]
     for a in range(2):
         for g in range(PASSES):
             for u in range(2):
-                nc.tensor.transpose(bank_of_pass[g][:, a, u, :], halves[:, a, g, u, :], ident[:])
+                nc.tensor.transpose(bank_of_pass[g][:, a, u, :], words[:, a, g, u, :], ident[:])
+    grouped = stage.tile([P, PASSES, PAIR, PACK], BF16, align_bytes=64)
     for g in range(PASSES):
-        grouped = stage.tile([P, PAIR, PACK], BF16, align_bytes=64)
-        nc.scalar.copy(
-            out=grouped[:].bitcast(F32).rearrange("p (a r) u -> p a r u", a=2),
-            in_=bank_of_pass[g][:].rearrange("p a u r -> p a r u"),
-        )
-        nc.vector.quantize_mx(
-            out=codes[:, g, :].bitcast(FP8X4),
-            scales=scales[:, g, :],
-            in_=grouped[:].rearrange("p r t -> p (r t)"),
-        )
+        side_by_side = grouped[:, g, :, :].bitcast(F32).rearrange("p (a r) u -> p a r u", a=2)
+        from_bank = bank_of_pass[g][:].rearrange("p a u r -> p a r u")
+        if vector_helps and g % 2 == 1:
+            nc.vector.tensor_copy(out=side_by_side, in_=from_bank)
+        else:
+            nc.scalar.copy(out=side_by_side, in_=from_bank)
+    return grouped
+
+
+def quantise_pair(nc, grouped, codes, scales):
+    nc.vector.quantize_mx(
+        out=codes[:].rearrange("p g r -> p (g r)").bitcast(FP8X4),
+        scales=scales[:].rearrange("p g r -> p (g r)"),
+        in_=grouped[:].rearrange("p g r t -> p (g r t)"),
+    )
 
 
 def tile_optimizedlinear_kernel(
@@ -58,8 +64,7 @@ def tile_optimizedlinear_kernel(
     nc = tc.nc
     with ExitStack() as ctx:
         keep = ctx.enter_context(tc.tile_pool(name="keep", bufs=1))
-        stage = ctx.enter_context(tc.tile_pool(name="stage", bufs=8))
-        sorting = ctx.enter_context(tc.tile_pool(name="sorting", bufs=2))
+        stage = ctx.enter_context(tc.tile_pool(name="stage", bufs=2))
         quantised = ctx.enter_context(tc.tile_pool(name="quantised", bufs=PERT_LAG + 2))
         banks = ctx.enter_context(tc.psum_pool(name="banks", bufs=4))
         sums = ctx.enter_context(tc.psum_pool(name="sums", bufs=4))
@@ -114,7 +119,8 @@ def tile_optimizedlinear_kernel(
         x_codes = [keep.tile([P, PASSES, PAIR], U32, name="x_codes%d" % h, align_bytes=64) for h in range(X_PAIRS)]
         x_scales = [keep.tile([P, PASSES, PAIR], U8, name="x_scales%d" % h, align_bytes=64) for h in range(X_PAIRS)]
         for h in range(X_PAIRS):
-            quantise_pair_along_k(nc, banks, stage, ident, by_half(x_raw[h]), x_codes[h], x_scales[h])
+            x_grouped = transpose_pair(nc, banks, stage, ident, words_by_half(x_raw[h]), True)
+            quantise_pair(nc, x_grouped, x_codes[h], x_scales[h])
 
         result = [
             [keep.tile([P, N_TILE], F32, name="result%d_%d" % (m, j)) for j in range(N_TILES)]
@@ -154,75 +160,72 @@ def tile_optimizedlinear_kernel(
         def pert_product(i, g_codes, g_scales):
             j = i // 2
             cols = slice(PAIR * (i % 2), PAIR * (i % 2 + 1))
-            for h in range(X_PAIRS):
-                pert = sums.tile([P, 2, PAIR], F32, name="sum")
-                for a in range(2):
-                    for g in range(PASSES):
-                        x_words, x_plane = x_operand(2 * h + a, g)
-                        nc.tensor.matmul_mx(
-                            out=pert[:, a, :],
-                            lhsT=x_words,
-                            lhsT_scale=x_plane,
-                            rhs=g_codes[:, g, :].bitcast(FP8X4),
-                            rhs_scale=g_scales[:, g, :],
-                            start=(g == 0),
-                            stop=(g == PASSES - 1),
-                        )
-                for a in range(2):
-                    m = 2 * h + a
-                    nc.vector.scalar_tensor_tensor(
-                        out=result[m][j][:, cols],
-                        in0=pert[:, a, :],
-                        scalar=neg_lr[:, m : m + 1],
-                        in1=result[m][j][:, cols],
-                        op0=MULT,
-                        op1=ADD,
+            for m in range(BATCH // P):
+                pert = sums.tile([P, PAIR], F32, name="sum")
+                for g in range(PASSES):
+                    x_words, x_plane = x_operand(m, g)
+                    nc.tensor.matmul_mx(
+                        out=pert[:],
+                        lhsT=x_words,
+                        lhsT_scale=x_plane,
+                        rhs=g_codes[:, g, :].bitcast(FP8X4),
+                        rhs_scale=g_scales[:, g, :],
+                        start=(g == 0),
+                        stop=(g == PASSES - 1),
                     )
-                    if i % 2 == 1:
-                        nc.sync.dma_start(
-                            out=out[P * m : P * (m + 1), N_TILE * j : N_TILE * (j + 1)], in_=result[m][j][:]
-                        )
+                nc.vector.scalar_tensor_tensor(
+                    out=result[m][j][:, cols],
+                    in0=pert[:],
+                    scalar=neg_lr[:, m : m + 1],
+                    in1=result[m][j][:, cols],
+                    op0=MULT,
+                    op1=ADD,
+                )
+                if i % 2 == 1:
+                    nc.sync.dma_start(out=out[P * m : P * (m + 1), N_TILE * j : N_TILE * (j + 1)], in_=result[m][j][:])
 
-        def rows_and_tile(half):
-            return (2 * (half % 2), 2 * (half % 2) + 1), half // 2
+        def rows_and_tile(portion):
+            return (2 * (portion % 2), 2 * (portion % 2) + 1), portion // 2
 
-        def bias_terms_of(half):
-            rows, j = rows_and_tile(half)
+        def bias_terms_of(portion):
+            rows, j = rows_and_tile(portion)
             for m in rows:
                 bias_terms(m, j)
 
-        def base_product_of(half):
-            rows, j = rows_and_tile(half)
+        def base_product_of(portion):
+            rows, j = rows_and_tile(portion)
             for m in rows:
                 base_product(m, j)
 
         def sort_words(i):
-            halves = sorting.tile([P, 2, PASSES, 2, P], F32, name="halves")
-            nc.vector.tensor_copy(out=halves[:, 0, :, :, :], in_=by_half(g_raw[i])[:, 0, :, :, :])
-            nc.scalar.copy(out=halves[:, 1, :, :, :], in_=by_half(g_raw[i])[:, 1, :, :, :])
-            return halves
+            sorted_words = stage.tile([P, 2, PASSES, 2, P], F32)
+            nc.vector.tensor_copy(out=sorted_words[:], in_=words_by_half(g_raw[i]))
+            return sorted_words
 
-        for half in range(BASE_LEAD):
-            bias_terms_of(half)
+        for portion in range(BASE_LEAD):
+            bias_terms_of(portion)
         base_product_of(0)
-        halves = sort_words(0)
-        for half in range(1, BASE_LEAD):
-            base_product_of(half)
+        sorted_next = sort_words(0)
+        for portion in range(1, BASE_LEAD):
+            base_product_of(portion)
 
+        g_grouped = None
         g_quantised = []
         for i in range(G_PAIRS + PERT_LAG):
-            half = i + BASE_LEAD
-            if half < HALVES:
-                bias_terms_of(half)
-            if i < G_PAIRS:
-                sorted_now = halves
-                if i + 1 < G_PAIRS:
-                    halves = sort_words(i + 1)
+            portion = i + BASE_LEAD
+            if portion < PORTIONS:
+                bias_terms_of(portion)
+            if 1 <= i <= G_PAIRS:
                 g_codes = quantised.tile([P, PASSES, PAIR], U32, align_bytes=64)
                 g_scales = quantised.tile([P, PASSES, PAIR], U8, align_bytes=64)
-                quantise_pair_along_k(nc, banks, stage, ident, sorted_now, g_codes, g_scales)
+                quantise_pair(nc, g_grouped, g_codes, g_scales)
                 g_quantised.append((g_codes, g_scales))
+            if i < G_PAIRS:
+                sorted_now = sorted_next
+                if i + 1 < G_PAIRS:
+                    sorted_next = sort_words(i + 1)
+                g_grouped = transpose_pair(nc, banks, stage, ident, sorted_now, False)
+            if portion < PORTIONS:
+                base_product_of(portion)
             if i >= PERT_LAG:
                 pert_product(i - PERT_LAG, g_quantised[i - PERT_LAG][0], g_quantised[i - PERT_LAG][1])
-            if half < HALVES:
-                base_product_of(half)

@@ -74,11 +74,6 @@ def tile_optimizedlinear_kernel(
         make_identity(nc, ident[:])
         w_planes = keep.tile([P, N], U8, align_bytes=64)
         nc.vector.memset(w_planes[:].bitcast(I32), 0)
-        lr_rows = keep.tile([P, BATCH], BF16)
-        vec_rows = keep.tile([P, N], BF16)
-        nc.vector.memset(lr_rows[:], 0.0)
-        nc.vector.memset(vec_rows[:], 0.0)
-        nc.vector.memset(lr_rows[0:1, :], 1.0)
 
         x_raw = [keep.tile([P, 2, K], BF16, name="x_raw%d" % h) for h in range(X_PAIRS)]
         g_raw = [keep.tile([P, 2, K], BF16, name="g_raw%d" % i) for i in range(G_PAIRS)]
@@ -87,6 +82,14 @@ def tile_optimizedlinear_kernel(
         def load_g(i):
             rows = prev_grad[PAIR * i : PAIR * (i + 1), :]
             nc.sync.dma_start(out=g_raw[i][:], in_=rows.rearrange("(a p) k -> p a k", p=P))
+
+        bias_all = [keep.tile([P, N_TILE], BF16, name="bias_all%d" % j) for j in range(N_TILES)]
+        grad_all = [keep.tile([P, N_TILE], BF16, name="grad_all%d" % j) for j in range(N_TILES)]
+
+        def load_vectors(j):
+            cols = slice(N_TILE * j, N_TILE * (j + 1))
+            nc.sync.dma_start(out=bias_all[j][:], in_=bias[cols].partition_broadcast(P))
+            nc.sync.dma_start(out=grad_all[j][:], in_=prev_bias_grad[cols].partition_broadcast(P))
 
         def load_w(j):
             cols = weight_words.rearrange("g p n t -> p g (n t)")[:, :, PACK * N_TILE * j : PACK * N_TILE * (j + 1)]
@@ -103,16 +106,13 @@ def tile_optimizedlinear_kernel(
             )
         for j in range(N_TILES):
             load_w(j)
+            load_vectors(j)
             load_g(2 * j)
             load_g(2 * j + 1)
 
-        nc.scalar.dma_start(out=vec_rows[0:1, :], in_=bias.unsqueeze(0))
-        nc.scalar.dma_start(out=vec_rows[32:33, :], in_=prev_bias_grad.unsqueeze(0))
-        nc.scalar.dma_start(out=lr_rows[32:33, :], in_=lr_samples.unsqueeze(0))
         lr_col = keep.tile([P, BATCH // P], BF16)
         with nc.allow_non_contiguous_dma(reason="512 learning rates, one batch row to a partition"):
             nc.scalar.dma_start(out=lr_col[:], in_=lr_samples.rearrange("(m p) -> p m", p=P))
-        nc.vector.tensor_scalar_mul(out=lr_rows[32:64, :], in0=lr_rows[32:64, :], scalar1=-1.0)
         neg_lr = keep.tile([P, BATCH // P], F32)
         nc.vector.tensor_scalar_mul(out=neg_lr[:], in0=lr_col[:], scalar1=-1.0)
 
@@ -132,15 +132,14 @@ def tile_optimizedlinear_kernel(
             return x_codes[m // 2][:, g, rows].bitcast(FP8X4), x_scales[m // 2][:, g, rows]
 
         def bias_terms(m, j):
-            terms = sums.tile([P, N_TILE], F32, name="sum")
-            nc.tensor.matmul(
-                out=terms[:],
-                lhsT=lr_rows[:, P * m : P * (m + 1)],
-                rhs=vec_rows[:, N_TILE * j : N_TILE * (j + 1)],
-                start=True,
-                stop=True,
+            nc.vector.scalar_tensor_tensor(
+                out=result[m][j][:],
+                in0=grad_all[j][:],
+                scalar=neg_lr[:, m : m + 1],
+                in1=bias_all[j][:],
+                op0=MULT,
+                op1=ADD,
             )
-            nc.scalar.copy(out=result[m][j][:], in_=terms[:])
 
         def base_product(m, j):
             base = sums.tile([P, N_TILE], F32, name="sum")
@@ -199,7 +198,10 @@ def tile_optimizedlinear_kernel(
 
         def sort_words(i):
             sorted_words = stage.tile([P, 2, PASSES, 2, P], F32)
-            nc.vector.tensor_copy(out=sorted_words[:], in_=words_by_half(g_raw[i]))
+            if i == 0:
+                nc.vector.tensor_copy(out=sorted_words[:], in_=words_by_half(g_raw[i]))
+            else:
+                nc.scalar.copy(out=sorted_words[:], in_=words_by_half(g_raw[i]))
             return sorted_words
 
         for portion in range(BASE_LEAD):

@@ -66,13 +66,21 @@ def tile_optimizedlinear_kernel(
         keep = ctx.enter_context(tc.tile_pool(name="keep", bufs=1))
         stage = ctx.enter_context(tc.tile_pool(name="stage", bufs=2))
         quantised = ctx.enter_context(tc.tile_pool(name="quantised", bufs=PERT_LAG + 2))
-        banks = ctx.enter_context(tc.psum_pool(name="banks", bufs=4))
-        sums = ctx.enter_context(tc.psum_pool(name="sums", bufs=4))
+        banks = ctx.enter_context(tc.psum_pool(name="banks", bufs=8))
+        sums = banks
         ctx.enter_context(tc.manual_schedule())
 
         ident = keep.tile([P, P], F32)
         make_identity(nc, ident[:])
         w_planes = keep.tile([P, N], U8, align_bytes=64)
+        vec_rows = keep.tile([P, N], BF16)
+        nc.vector.memset(vec_rows[:], 0.0)
+        pick_bias = keep.tile([P, P], BF16)
+        pick_grad = keep.tile([P, P], BF16)
+        nc.vector.memset(pick_bias[:], 0.0)
+        nc.vector.memset(pick_grad[:], 0.0)
+        nc.vector.memset(pick_bias[0:1, :], 1.0)
+        nc.vector.memset(pick_grad[32:33, :], 1.0)
         nc.vector.memset(w_planes[:].bitcast(I32), 0)
 
         x_raw = [keep.tile([P, 2, K], BF16, name="x_raw%d" % h) for h in range(X_PAIRS)]
@@ -86,10 +94,12 @@ def tile_optimizedlinear_kernel(
         bias_all = [keep.tile([P, N_TILE], BF16, name="bias_all%d" % j) for j in range(N_TILES)]
         grad_all = [keep.tile([P, N_TILE], BF16, name="grad_all%d" % j) for j in range(N_TILES)]
 
-        def load_vectors(j):
+        def spread(j):
             cols = slice(N_TILE * j, N_TILE * (j + 1))
-            nc.sync.dma_start(out=bias_all[j][:], in_=bias[cols].partition_broadcast(P))
-            nc.sync.dma_start(out=grad_all[j][:], in_=prev_bias_grad[cols].partition_broadcast(P))
+            for selector, everywhere in ((pick_bias, bias_all[j]), (pick_grad, grad_all[j])):
+                repeated = banks.tile([P, N_TILE], F32, name="bank")
+                nc.tensor.matmul(out=repeated[:], lhsT=selector[:], rhs=vec_rows[:, cols], start=True, stop=True)
+                nc.scalar.copy(out=everywhere[:], in_=repeated[:])
 
         def load_w(j):
             cols = weight_words.rearrange("g p n t -> p g (n t)")[:, :, PACK * N_TILE * j : PACK * N_TILE * (j + 1)]
@@ -106,10 +116,11 @@ def tile_optimizedlinear_kernel(
             )
         for j in range(N_TILES):
             load_w(j)
-            load_vectors(j)
             load_g(2 * j)
             load_g(2 * j + 1)
 
+        nc.scalar.dma_start(out=vec_rows[0:1, :], in_=bias.unsqueeze(0))
+        nc.scalar.dma_start(out=vec_rows[32:33, :], in_=prev_bias_grad.unsqueeze(0))
         lr_col = keep.tile([P, BATCH // P], BF16)
         with nc.allow_non_contiguous_dma(reason="512 learning rates, one batch row to a partition"):
             nc.scalar.dma_start(out=lr_col[:], in_=lr_samples.rearrange("(m p) -> p m", p=P))
@@ -118,10 +129,6 @@ def tile_optimizedlinear_kernel(
 
         x_codes = [keep.tile([P, PASSES, PAIR], U32, name="x_codes%d" % h, align_bytes=64) for h in range(X_PAIRS)]
         x_scales = [keep.tile([P, PASSES, PAIR], U8, name="x_scales%d" % h, align_bytes=64) for h in range(X_PAIRS)]
-        for h in range(X_PAIRS):
-            x_grouped = transpose_pair(nc, banks, stage, ident, words_by_half(x_raw[h]), True)
-            quantise_pair(nc, x_grouped, x_codes[h], x_scales[h])
-
         result = [
             [keep.tile([P, N_TILE], F32, name="result%d_%d" % (m, j)) for j in range(N_TILES)]
             for m in range(BATCH // P)
@@ -142,7 +149,7 @@ def tile_optimizedlinear_kernel(
             )
 
         def base_product(m, j):
-            base = sums.tile([P, N_TILE], F32, name="sum")
+            base = sums.tile([P, N_TILE], F32, name="bank")
             for g in range(PASSES):
                 x_words, x_plane = x_operand(m, g)
                 nc.tensor.matmul_mx(
@@ -160,7 +167,7 @@ def tile_optimizedlinear_kernel(
             j = i // 2
             cols = slice(PAIR * (i % 2), PAIR * (i % 2 + 1))
             for m in range(BATCH // P):
-                pert = sums.tile([P, PAIR], F32, name="sum")
+                pert = sums.tile([P, PAIR], F32, name="bank")
                 for g in range(PASSES):
                     x_words, x_plane = x_operand(m, g)
                     nc.tensor.matmul_mx(
@@ -204,8 +211,13 @@ def tile_optimizedlinear_kernel(
                 nc.scalar.copy(out=sorted_words[:], in_=words_by_half(g_raw[i]))
             return sorted_words
 
-        for portion in range(BASE_LEAD):
-            bias_terms_of(portion)
+        for h in range(X_PAIRS):
+            x_grouped = transpose_pair(nc, banks, stage, ident, words_by_half(x_raw[h]), True)
+            quantise_pair(nc, x_grouped, x_codes[h], x_scales[h])
+            spread(2 * h)
+            spread(2 * h + 1)
+            bias_terms_of(h)
+
         base_product_of(0)
         sorted_next = sort_words(0)
         for portion in range(1, BASE_LEAD):

@@ -23,7 +23,7 @@ G_PAIRS = N // PAIR
 N_TILE = 512
 N_TILES = N // N_TILE
 PORTIONS = 2 * N_TILES
-BASE_LEAD = 2
+BASE_LEAD = 3
 PERT_LAG = 2
 
 FLOPS = 2 * 2 * BATCH * K * N
@@ -114,10 +114,15 @@ def tile_optimizedlinear_kernel(
                 out=w_planes[32 * quadrant : 32 * quadrant + 16, :].bitcast(I32),
                 in_=weight_scales[:, 4 * quadrant : 4 * quadrant + 4, :].bitcast(I32),
             )
-        for j in range(N_TILES):
-            load_w(j)
-            load_g(2 * j)
-            load_g(2 * j + 1)
+        load_w(0)
+        load_g(0)
+        load_w(1)
+        for i in range(G_PAIRS):
+            portion = i + BASE_LEAD
+            if portion < PORTIONS and portion % 2 == 0:
+                load_w(portion // 2)
+            if i + 1 < G_PAIRS:
+                load_g(i + 1)
 
         nc.scalar.dma_start(out=vec_rows[0:1, :], in_=bias.unsqueeze(0))
         nc.scalar.dma_start(out=vec_rows[32:33, :], in_=prev_bias_grad.unsqueeze(0))
@@ -205,7 +210,7 @@ def tile_optimizedlinear_kernel(
 
         def sort_words(i):
             sorted_words = stage.tile([P, 2, PASSES, 2, P], F32)
-            if i == 0:
+            if i % 2 == 0:
                 nc.vector.tensor_copy(out=sorted_words[:], in_=words_by_half(g_raw[i]))
             else:
                 nc.scalar.copy(out=sorted_words[:], in_=words_by_half(g_raw[i]))
@@ -219,8 +224,10 @@ def tile_optimizedlinear_kernel(
             bias_terms_of(h)
 
         base_product_of(0)
+        base_product_of(1)
         sorted_next = sort_words(0)
-        for portion in range(1, BASE_LEAD):
+        for portion in range(2, BASE_LEAD):
+            bias_terms_of(portion)
             base_product_of(portion)
 
         g_grouped = None

@@ -23,8 +23,9 @@ G_PAIRS = N // PAIR
 N_TILE = 512
 N_TILES = N // N_TILE
 PORTIONS = 2 * N_TILES
-BASE_LEAD = 3
-PERT_LAG = 2
+BASE_LEAD = 4
+RUN = 2
+RUNS = G_PAIRS // RUN
 
 FLOPS = 2 * 2 * BATCH * K * N
 
@@ -65,7 +66,7 @@ def tile_optimizedlinear_kernel(
     with ExitStack() as ctx:
         keep = ctx.enter_context(tc.tile_pool(name="keep", bufs=1))
         stage = ctx.enter_context(tc.tile_pool(name="stage", bufs=2))
-        quantised = ctx.enter_context(tc.tile_pool(name="quantised", bufs=PERT_LAG + 2))
+        quantised = ctx.enter_context(tc.tile_pool(name="quantised", bufs=2 * RUN))
         banks = ctx.enter_context(tc.psum_pool(name="banks", bufs=8))
         sums = banks
         ctx.enter_context(tc.manual_schedule())
@@ -115,14 +116,12 @@ def tile_optimizedlinear_kernel(
                 in_=weight_scales[:, 4 * quadrant : 4 * quadrant + 4, :].bitcast(I32),
             )
         load_w(0)
-        load_g(0)
         load_w(1)
-        for i in range(G_PAIRS):
-            portion = i + BASE_LEAD
-            if portion < PORTIONS and portion % 2 == 0:
-                load_w(portion // 2)
-            if i + 1 < G_PAIRS:
-                load_g(i + 1)
+        for run in range(RUNS):
+            load_g(RUN * run)
+            load_g(RUN * run + 1)
+            if run + 2 < N_TILES:
+                load_w(run + 2)
 
         nc.scalar.dma_start(out=vec_rows[0:1, :], in_=bias.unsqueeze(0))
         nc.scalar.dma_start(out=vec_rows[32:33, :], in_=prev_bias_grad.unsqueeze(0))
@@ -225,28 +224,36 @@ def tile_optimizedlinear_kernel(
 
         base_product_of(0)
         base_product_of(1)
-        sorted_next = sort_words(0)
-        for portion in range(2, BASE_LEAD):
-            bias_terms_of(portion)
-            base_product_of(portion)
+        bias_terms_of(2)
+        bias_terms_of(3)
+        sorted_words_of = {0: sort_words(0), 1: sort_words(1)}
+        base_product_of(2)
+        base_product_of(3)
 
-        g_grouped = None
-        g_quantised = []
-        for i in range(G_PAIRS + PERT_LAG):
-            portion = i + BASE_LEAD
-            if portion < PORTIONS:
+        def quantise_g(g_grouped):
+            g_codes = quantised.tile([P, PASSES, PAIR], U32, align_bytes=64)
+            g_scales = quantised.tile([P, PASSES, PAIR], U8, align_bytes=64)
+            quantise_pair(nc, g_grouped, g_codes, g_scales)
+            return g_codes, g_scales
+
+        g_quantised = {}
+        for run in range(RUNS + 1):
+            first = RUN * run
+            portions = [p for p in (BASE_LEAD + 2 * run, BASE_LEAD + 2 * run + 1) if p < PORTIONS]
+            for portion in portions:
                 bias_terms_of(portion)
-            if 1 <= i <= G_PAIRS:
-                g_codes = quantised.tile([P, PASSES, PAIR], U32, align_bytes=64)
-                g_scales = quantised.tile([P, PASSES, PAIR], U8, align_bytes=64)
-                quantise_pair(nc, g_grouped, g_codes, g_scales)
-                g_quantised.append((g_codes, g_scales))
-            if i < G_PAIRS:
-                sorted_now = sorted_next
-                if i + 1 < G_PAIRS:
-                    sorted_next = sort_words(i + 1)
-                g_grouped = transpose_pair(nc, banks, stage, ident, sorted_now, False)
-            if portion < PORTIONS:
+            g_grouped = []
+            if run < RUNS:
+                for i in (first, first + 1):
+                    g_grouped.append(transpose_pair(nc, banks, stage, ident, sorted_words_of[i], False))
+                if run + 1 < RUNS:
+                    for i in (first + RUN, first + RUN + 1):
+                        sorted_words_of[i] = sort_words(i)
+            for portion in portions:
                 base_product_of(portion)
-            if i >= PERT_LAG:
-                pert_product(i - PERT_LAG, g_quantised[i - PERT_LAG][0], g_quantised[i - PERT_LAG][1])
+            for n in range(RUN):
+                if run < RUNS:
+                    g_quantised[first + n] = quantise_g(g_grouped[n])
+                if run >= 1:
+                    i = first - RUN + n
+                    pert_product(i, g_quantised[i][0], g_quantised[i][1])

@@ -40,7 +40,7 @@ def transpose_pair(nc, banks, stage, ident, words, vector_helps):
         for g in range(PASSES):
             for u in range(2):
                 nc.tensor.transpose(bank_of_pass[g][:, a, u, :], words[:, a, g, u, :], ident[:])
-    grouped = stage.tile([P, PASSES, PAIR, PACK], BF16, align_bytes=64)
+    grouped = stage.tile([P, PASSES, PAIR, PACK], BF16, align_bytes=256)
     for g in range(PASSES):
         side_by_side = grouped[:, g, :, :].bitcast(F32).rearrange("p (a r) u -> p a r u", a=2)
         from_bank = bank_of_pass[g][:].rearrange("p a u r -> p a r u")
@@ -73,7 +73,7 @@ def tile_optimizedlinear_kernel(
 
         ident = keep.tile([P, P], F32)
         make_identity(nc, ident[:])
-        w_planes = keep.tile([P, N], U8, align_bytes=64)
+        w_planes = keep.tile([P, N], U8, align_bytes=256)
         vec_rows = keep.tile([P, N], BF16)
         nc.vector.memset(vec_rows[:], 0.0)
         pick_bias = keep.tile([P, P], BF16)
@@ -86,7 +86,7 @@ def tile_optimizedlinear_kernel(
 
         x_raw = [keep.tile([P, 2, K], BF16, name="x_raw%d" % h) for h in range(X_PAIRS)]
         g_raw = [keep.tile([P, 2, K], BF16, name="g_raw%d" % i) for i in range(G_PAIRS)]
-        w_words = [keep.tile([P, PASSES, N_TILE], U32, name="w_words%d" % j, align_bytes=64) for j in range(N_TILES)]
+        w_words = [keep.tile([P, PASSES, N_TILE], U32, name="w_words%d" % j, align_bytes=256) for j in range(N_TILES)]
 
         def load_g(i):
             rows = prev_grad[PAIR * i : PAIR * (i + 1), :]
@@ -131,8 +131,8 @@ def tile_optimizedlinear_kernel(
         neg_lr = keep.tile([P, BATCH // P], F32)
         nc.vector.tensor_scalar_mul(out=neg_lr[:], in0=lr_col[:], scalar1=-1.0)
 
-        x_codes = [keep.tile([P, PASSES, PAIR], U32, name="x_codes%d" % h, align_bytes=64) for h in range(X_PAIRS)]
-        x_scales = [keep.tile([P, PASSES, PAIR], U8, name="x_scales%d" % h, align_bytes=64) for h in range(X_PAIRS)]
+        x_codes = [keep.tile([P, PASSES, PAIR], U32, name="x_codes%d" % h, align_bytes=256) for h in range(X_PAIRS)]
+        x_scales = [keep.tile([P, PASSES, PAIR], U8, name="x_scales%d" % h, align_bytes=256) for h in range(X_PAIRS)]
         result = [
             [keep.tile([P, N_TILE], F32, name="result%d_%d" % (m, j)) for j in range(N_TILES)]
             for m in range(BATCH // P)
@@ -231,8 +231,8 @@ def tile_optimizedlinear_kernel(
         base_product_of(3)
 
         def quantise_g(g_grouped):
-            g_codes = quantised.tile([P, PASSES, PAIR], U32, align_bytes=64)
-            g_scales = quantised.tile([P, PASSES, PAIR], U8, align_bytes=64)
+            g_codes = quantised.tile([P, PASSES, PAIR], U32, align_bytes=256)
+            g_scales = quantised.tile([P, PASSES, PAIR], U8, align_bytes=256)
             quantise_pair(nc, g_grouped, g_codes, g_scales)
             return g_codes, g_scales
 

from contextlib import ExitStack

import concourse.mybir as mybir
from concourse.masks import make_identity

F32 = mybir.dt.float32
BF16 = mybir.dt.bfloat16
I32 = mybir.dt.int32
U32 = mybir.dt.uint32
U8 = mybir.dt.uint8
FP8X4 = mybir.dt.float8_e4m3fn_x4
ADD = mybir.AluOpType.add
MULT = mybir.AluOpType.mult

P = 128
PACK = 4
K_PASS = P * PACK
BATCH, K, N = 512, 2048, 2048
PASSES = K // K_PASS
PAIR = 2 * P
X_PAIRS = BATCH // PAIR
G_PAIRS = N // PAIR
N_TILE = 512
N_TILES = N // N_TILE
PORTIONS = 2 * N_TILES
BASE_LEAD = 4
RUN = 2
RUNS = G_PAIRS // RUN

FLOPS = 2 * 2 * BATCH * K * N


def words_by_half(raw):
    return raw[:].bitcast(F32).rearrange("p a (g i u) -> p a g u i", g=PASSES, u=2)


def transpose_pair(nc, banks, stage, ident, words, vector_helps):
    bank_of_pass = [banks.tile([P, 2, 2, P], F32, name="bank") for g in range(PASSES)]
    for a in range(2):
        for g in range(PASSES):
            for u in range(2):
                nc.tensor.transpose(bank_of_pass[g][:, a, u, :], words[:, a, g, u, :], ident[:])
    grouped = stage.tile([P, PASSES, PAIR, PACK], BF16, align_bytes=256)
    for g in range(PASSES):
        side_by_side = grouped[:, g, :, :].bitcast(F32).rearrange("p (a r) u -> p a r u", a=2)
        from_bank = bank_of_pass[g][:].rearrange("p a u r -> p a r u")
        if vector_helps and g % 2 == 1:
            nc.vector.tensor_copy(out=side_by_side, in_=from_bank)
        else:
            nc.scalar.copy(out=side_by_side, in_=from_bank)
    return grouped


def quantise_pair(nc, grouped, codes, scales):
    nc.vector.quantize_mx(
        out=codes[:].rearrange("p g r -> p (g r)").bitcast(FP8X4),
        scales=scales[:].rearrange("p g r -> p (g r)"),
        in_=grouped[:].rearrange("p g r t -> p (g r t)"),
    )


def tile_optimizedlinear_kernel(
    tc, input_data, weight_words, weight_scales, bias, prev_grad, prev_bias_grad, lr_samples, out
):
    nc = tc.nc
    with ExitStack() as ctx:
        keep = ctx.enter_context(tc.tile_pool(name="keep", bufs=1))
        stage = ctx.enter_context(tc.tile_pool(name="stage", bufs=2))
        quantised = ctx.enter_context(tc.tile_pool(name="quantised", bufs=2 * RUN))
        banks = ctx.enter_context(tc.psum_pool(name="banks", bufs=8))
        sums = banks
        ctx.enter_context(tc.manual_schedule())

        ident = keep.tile([P, P], F32)
        make_identity(nc, ident[:])
        w_planes = keep.tile([P, N], U8, align_bytes=256)
        vec_rows = keep.tile([P, N], BF16)
        nc.vector.memset(vec_rows[:], 0.0)
        pick_bias = keep.tile([P, P], BF16)
        pick_grad = keep.tile([P, P], BF16)
        nc.vector.memset(pick_bias[:], 0.0)
        nc.vector.memset(pick_grad[:], 0.0)
        nc.vector.memset(pick_bias[0:1, :], 1.0)
        nc.vector.memset(pick_grad[32:33, :], 1.0)
        nc.vector.memset(w_planes[:].bitcast(I32), 0)

        x_raw = [keep.tile([P, 2, K], BF16, name="x_raw%d" % h) for h in range(X_PAIRS)]
        g_raw = [keep.tile([P, 2, K], BF16, name="g_raw%d" % i) for i in range(G_PAIRS)]
        w_words = [keep.tile([P, PASSES, N_TILE], U32, name="w_words%d" % j, align_bytes=256) for j in range(N_TILES)]

        def load_g(i):
            rows = prev_grad[PAIR * i : PAIR * (i + 1), :]
            nc.sync.dma_start(out=g_raw[i][:], in_=rows.rearrange("(a p) k -> p a k", p=P))

        bias_all = [keep.tile([P, N_TILE], BF16, name="bias_all%d" % j) for j in range(N_TILES)]
        grad_all = [keep.tile([P, N_TILE], BF16, name="grad_all%d" % j) for j in range(N_TILES)]

        def spread(j):
            cols = slice(N_TILE * j, N_TILE * (j + 1))
            for selector, everywhere in ((pick_bias, bias_all[j]), (pick_grad, grad_all[j])):
                repeated = banks.tile([P, N_TILE], F32, name="bank")
                nc.tensor.matmul(out=repeated[:], lhsT=selector[:], rhs=vec_rows[:, cols], start=True, stop=True)
                nc.scalar.copy(out=everywhere[:], in_=repeated[:])

        def load_w(j):
            cols = weight_words.rearrange("g p n t -> p g (n t)")[:, :, PACK * N_TILE * j : PACK * N_TILE * (j + 1)]
            nc.sync.dma_start(out=w_words[j][:].bitcast(I32), in_=cols.bitcast(I32))

        for h in range(X_PAIRS):
            for a in range(2):
                m = 2 * h + a
                nc.sync.dma_start(out=x_raw[h][:, a, :], in_=input_data[P * m : P * (m + 1), :])
        for quadrant in range(4):
            nc.sync.dma_start(
                out=w_planes[32 * quadrant : 32 * quadrant + 16, :].bitcast(I32),
                in_=weight_scales[:, 4 * quadrant : 4 * quadrant + 4, :].bitcast(I32),
            )
        load_w(0)
        load_w(1)
        for run in range(RUNS):
            load_g(RUN * run)
            load_g(RUN * run + 1)
            if run + 2 < N_TILES:
                load_w(run + 2)

        nc.scalar.dma_start(out=vec_rows[0:1, :], in_=bias.unsqueeze(0))
        nc.scalar.dma_start(out=vec_rows[32:33, :], in_=prev_bias_grad.unsqueeze(0))
        lr_col = keep.tile([P, BATCH // P], BF16)
        with nc.allow_non_contiguous_dma(reason="512 learning rates, one batch row to a partition"):
            nc.scalar.dma_start(out=lr_col[:], in_=lr_samples.rearrange("(m p) -> p m", p=P))
        neg_lr = keep.tile([P, BATCH // P], F32)
        nc.vector.tensor_scalar_mul(out=neg_lr[:], in0=lr_col[:], scalar1=-1.0)

        x_codes = [keep.tile([P, PASSES, PAIR], U32, name="x_codes%d" % h, align_bytes=256) for h in range(X_PAIRS)]
        x_scales = [keep.tile([P, PASSES, PAIR], U8, name="x_scales%d" % h, align_bytes=256) for h in range(X_PAIRS)]
        result = [
            [keep.tile([P, N_TILE], F32, name="result%d_%d" % (m, j)) for j in range(N_TILES)]
            for m in range(BATCH // P)
        ]

        def x_operand(m, g):
            rows = slice(P * (m % 2), P * (m % 2 + 1))
            return x_codes[m // 2][:, g, rows].bitcast(FP8X4), x_scales[m // 2][:, g, rows]

        def bias_terms(m, j):
            nc.vector.scalar_tensor_tensor(
                out=result[m][j][:],
                in0=grad_all[j][:],
                scalar=neg_lr[:, m : m + 1],
                in1=bias_all[j][:],
                op0=MULT,
                op1=ADD,
            )

        def base_product(m, j):
            base = sums.tile([P, N_TILE], F32, name="bank")
            for g in range(PASSES):
                x_words, x_plane = x_operand(m, g)
                nc.tensor.matmul_mx(
                    out=base[:],
                    lhsT=x_words,
                    lhsT_scale=x_plane,
                    rhs=w_words[j][:, g, :].bitcast(FP8X4),
                    rhs_scale=w_planes[4 * g : P, N_TILE * j : N_TILE * (j + 1)],
                    start=(g == 0),
                    stop=(g == PASSES - 1),
                )
            nc.vector.tensor_tensor(out=result[m][j][:], in0=base[:], in1=result[m][j][:], op=ADD)

        def pert_product(i, g_codes, g_scales):
            j = i // 2
            cols = slice(PAIR * (i % 2), PAIR * (i % 2 + 1))
            for m in range(BATCH // P):
                pert = sums.tile([P, PAIR], F32, name="bank")
                for g in range(PASSES):
                    x_words, x_plane = x_operand(m, g)
                    nc.tensor.matmul_mx(
                        out=pert[:],
                        lhsT=x_words,
                        lhsT_scale=x_plane,
                        rhs=g_codes[:, g, :].bitcast(FP8X4),
                        rhs_scale=g_scales[:, g, :],
                        start=(g == 0),
                        stop=(g == PASSES - 1),
                    )
                nc.vector.scalar_tensor_tensor(
                    out=result[m][j][:, cols],
                    in0=pert[:],
                    scalar=neg_lr[:, m : m + 1],
                    in1=result[m][j][:, cols],
                    op0=MULT,
                    op1=ADD,
                )
                if i % 2 == 1:
                    nc.sync.dma_start(out=out[P * m : P * (m + 1), N_TILE * j : N_TILE * (j + 1)], in_=result[m][j][:])

        def rows_and_tile(portion):
            return (2 * (portion % 2), 2 * (portion % 2) + 1), portion // 2

        def bias_terms_of(portion):
            rows, j = rows_and_tile(portion)
            for m in rows:
                bias_terms(m, j)

        def base_product_of(portion):
            rows, j = rows_and_tile(portion)
            for m in rows:
                base_product(m, j)

        def sort_words(i):
            sorted_words = stage.tile([P, 2, PASSES, 2, P], F32)
            if i % 2 == 0:
                nc.vector.tensor_copy(out=sorted_words[:], in_=words_by_half(g_raw[i]))
            else:
                nc.scalar.copy(out=sorted_words[:], in_=words_by_half(g_raw[i]))
            return sorted_words

        for h in range(X_PAIRS):
            x_grouped = transpose_pair(nc, banks, stage, ident, words_by_half(x_raw[h]), True)
            quantise_pair(nc, x_grouped, x_codes[h], x_scales[h])
            spread(2 * h)
            spread(2 * h + 1)
            bias_terms_of(h)

        base_product_of(0)
        base_product_of(1)
        bias_terms_of(2)
        bias_terms_of(3)
        sorted_words_of = {0: sort_words(0), 1: sort_words(1)}
        base_product_of(2)
        base_product_of(3)

        def quantise_g(g_grouped):
            g_codes = quantised.tile([P, PASSES, PAIR], U32, align_bytes=256)
            g_scales = quantised.tile([P, PASSES, PAIR], U8, align_bytes=256)
            quantise_pair(nc, g_grouped, g_codes, g_scales)
            return g_codes, g_scales

        g_quantised = {}
        for run in range(RUNS + 1):
            first = RUN * run
            portions = [p for p in (BASE_LEAD + 2 * run, BASE_LEAD + 2 * run + 1) if p < PORTIONS]
            for portion in portions:
                bias_terms_of(portion)
            g_grouped = []
            if run < RUNS:
                for i in (first, first + 1):
                    g_grouped.append(transpose_pair(nc, banks, stage, ident, sorted_words_of[i], False))
                if run + 1 < RUNS:
                    for i in (first + RUN, first + RUN + 1):
                        sorted_words_of[i] = sort_words(i)
            for portion in portions:
                base_product_of(portion)
            for n in range(RUN):
                if run < RUNS:
                    g_quantised[first + n] = quantise_g(g_grouped[n])
                if run >= 1:
                    i = first - RUN + n
                    pert_product(i, g_quantised[i][0], g_quantised[i][1])
